import numpy as np
import ml_dtypes


def mxq(x, axis, fmt="e4m3"):
    dtype, down = {"e4m3": (ml_dtypes.float8_e4m3fn, 7), "e5m2": (ml_dtypes.float8_e5m2, 14)}[fmt]
    v = np.moveaxis(np.asarray(x, np.float32).astype(ml_dtypes.bfloat16).astype(np.float64), axis, -1)
    blocks = v.reshape(v.shape[:-1] + (-1, 32))
    amax = np.abs(blocks).max(-1, keepdims=True)
    byte = np.maximum(np.where(amax > 0, np.frexp(amax)[1] - 1 + 127, 0) - down, 1)
    scale = np.exp2(byte - 127.0)
    codes = (blocks / scale).astype(np.float32).astype(dtype).astype(np.float64)
    return np.moveaxis((codes * scale).reshape(v.shape), -1, axis)


WIDE = False


def mx_kscale(k):
    if not WIDE:
        return np.ones(k)
    levels = np.array([10, -10, 5, -5, 0])
    if k % 512:
        return np.exp2(np.random.permutation(np.resize(levels, k // 32))).repeat(32)
    a = np.empty((k // 512, 16))
    for p in range(k // 512):
        a[p, :8] = np.random.permutation(np.resize(levels, 8))
        for g in range(8):
            far = levels[np.abs(levels - a[p, g]) >= 10]
            a[p, g + 8] = far[np.random.randint(len(far))]
    return np.exp2(a.ravel()).repeat(32)


BF16 = ml_dtypes.bfloat16


def bf(x):
    return np.asarray(x, np.float32).astype(BF16)


def f64(x):
    return np.asarray(x).astype(np.float64)


B, CIN, COUT, T, R, C = 2, 1024, 128, 8, 16, 16


def setup_inputs():
    s = mx_kscale(CIN)
    x = np.random.standard_normal((B, CIN, T, R, C)) * s[None, :, None, None, None]
    W = np.random.standard_normal((7 * COUT, CIN)) * 0.5 / np.sqrt(CIN) / s[None, :]
    return {"x": bf(x), "W": bf(W)}


def _shift(a, axis, d):
    pads = [(0, 0)] * a.ndim
    idx = [slice(None)] * a.ndim
    if d > 0:
        pads[axis] = (1, 0)
        idx[axis] = slice(0, -1)
    else:
        pads[axis] = (0, 1)
        idx[axis] = slice(1, None)
    return np.pad(a, pads)[tuple(idx)]


def reference(x, W):
    cout = W.shape[0] // 7
    xq = mxq(f64(x), 1, "e4m3")
    Wq = mxq(f64(W), 1, "e4m3")
    all_out = xq.transpose(0, 2, 3, 4, 1) @ Wq.T
    a = all_out.reshape(*all_out.shape[:4], 7, cout)
    out = a[..., 0, :]
    out = out + _shift(a[..., 1, :], 1, +1)
    out = out + _shift(a[..., 2, :], 1, -1)
    out = out + _shift(a[..., 3, :], 2, +1)
    out = out + _shift(a[..., 4, :], 2, -1)
    out = out + _shift(a[..., 5, :], 3, +1)
    out = out + _shift(a[..., 6, :], 3, -1)
    return np.transpose(out, (0, 4, 1, 2, 3))

@@ -1,0 +1,321 @@
+from contextlib import ExitStack
+
+import concourse.mybir as mybir
+from concourse.masks import make_identity
+
+FLOPS = 2 * 4096 * 1024 * 896
+
+F32 = mybir.dt.float32
+BF16 = mybir.dt.bfloat16
+U32 = mybir.dt.uint32
+U8 = mybir.dt.uint8
+FP8X4 = mybir.dt.float8_e4m3fn_x4
+ADD = mybir.AluOpType.add
+
+P = 128
+PACK = 4
+G = 2
+SLICE = 256
+CHUNK = 512
+N_PAIRS = 8
+LINE = 16
+BASE = 16
+SPLIT_HEAD = 256
+SPLIT = 320
+W_FIRST = (6, 5, 4, 0, 3)
+W_LATER = (2, 1)
+PINNED = True
+HEAD_PAIRS = 3
+FINE_PAIRS = 3
+W_ON_VECTOR = 0
+HEAD_UNITS = [(0, 0, 0, SLICE), (0, 0, SLICE, SLICE), (0, 1, 0, CHUNK)]
+UNITS = [(q, g, 0, CHUNK) for q in range(1, N_PAIRS) for g in range(G)]
+
+
+def tile_stackeddirectionalconv3d_t_kernel(tc, x, W, out):
+    nc = tc.nc
+    with ExitStack() as ctx:
+        if PINNED:
+            ctx.enter_context(tc.manual_schedule())
+        keep = ctx.enter_context(tc.tile_pool(name="keep", bufs=1))
+        stage = ctx.enter_context(tc.tile_pool(name="stage", bufs=3))
+        psum = ctx.enter_context(tc.psum_pool(name="psum", bufs=1))
+
+        x_codes = keep.tile([P, N_PAIRS, G, CHUNK], U32, name="x_codes", align_bytes=64)
+        x_scales = keep.tile([P, N_PAIRS, G, CHUNK], U8, name="x_scales", align_bytes=64)
+        w_codes = keep.tile([P, 7, G * P], U32, name="w_codes", align_bytes=64)
+        w_scales = keep.tile([P, 7, G * P], U8, name="w_scales", align_bytes=64)
+        zero_bf = keep.tile([P, P * PACK], BF16, name="zero_bf", align_bytes=64)
+        zero_codes = keep.tile([P, P], U32, name="zero_codes", align_bytes=64)
+        zero_scales = keep.tile([P, P], U8, name="zero_scales", align_bytes=64)
+        ident = keep.tile([P, P], F32, name="ident")
+        res = keep.tile([P, N_PAIRS, CHUNK], F32, name="res")
+
+        w_raw = {}
+
+        def load_w(k):
+            w_raw[k] = keep.tile([P, 1024], BF16, name="w_raw%d" % k)
+            nc.sync.dma_start(out=w_raw[k][:], in_=W[P * k : P * (k + 1), :])
+
+        x_raw = {}
+
+        def load_x(unit):
+            q, g, c0, n = unit
+            if q < FINE_PAIRS:
+                x_raw[unit] = keep.tile([P, PACK, n], BF16, name="x_raw_%d_%d_%d" % (q, g, c0))[:]
+            else:
+                if g == 0:
+                    x_raw[q] = keep.tile([P, G, PACK, CHUNK], BF16, name="x_raw_%d" % q)
+                x_raw[unit] = x_raw[q][:, g, :, :]
+            b, qq = divmod(q, 4)
+            xb = x[b].rearrange("k t r c -> k (t r c)")
+            rows = xb[512 * g : 512 * g + 512, CHUNK * qq + c0 : CHUNK * qq + c0 + n]
+            nc.sync.dma_start(out=x_raw[unit], in_=rows.rearrange("(p e) w -> p e w", e=PACK))
+
+        for k in W_FIRST:
+            load_w(k)
+        load_x(HEAD_UNITS[0])
+        for k in W_LATER:
+            load_w(k)
+        for unit in HEAD_UNITS[1:] + UNITS:
+            load_x(unit)
+
+        def lines(ap):
+            return ap.rearrange("p (l c) -> p l c", c=LINE)
+
+        make_identity(nc, ident[:])
+        nc.vector.memset(zero_bf[:], 0.0)
+        nc.vector.memset(lines(res[:, N_PAIRS - 1, :])[:, :, LINE - 1 : LINE], 0.0)
+        nc.vector.quantize_mx(out=zero_codes[:].bitcast(FP8X4), scales=zero_scales[:], in_=zero_bf[:])
+
+        def bank(i, name):
+            return psum.tile([P, 512], F32, name=name, tag="bank%d" % i)
+
+        wt = {}
+
+        def w_transposes(i, k):
+            words = w_raw[k][:].bitcast(F32)
+            wt[k] = bank(i, "wt%d" % k)
+            for j in range(4):
+                g, u = divmod(j, 2)
+                nc.tensor.transpose(
+                    wt[k][:, P * j : P * (j + 1)], words[:, 256 * g + u : 256 * (g + 1) : 2], ident[:]
+                )
+
+        w_grouped = {}
+
+        def w_copy(i, k):
+            w_grouped[k] = stage.tile([P, G * P * PACK], BF16, name="w_grouped", align_bytes=64)
+            dst = w_grouped[k][:].bitcast(F32).rearrange("p (g o u) -> p g o u", g=G, u=2)
+            src = wt[k][:].rearrange("p (g u o) -> p g o u", g=G, u=2)
+            if W_ON_VECTOR and i % W_ON_VECTOR == W_ON_VECTOR - 1:
+                nc.vector.tensor_copy(out=dst, in_=src)
+            else:
+                nc.scalar.copy(out=dst, in_=src)
+
+        def w_quant(k):
+            nc.vector.quantize_mx(
+                out=w_codes[:, k, :].bitcast(FP8X4), scales=w_scales[:, k, :], in_=w_grouped[k][:]
+            )
+
+        grouped = {}
+
+        def runs4(ap, order):
+            return ap.rearrange(order, i=4)
+
+        def x_copy(unit):
+            q, g, c0, n = unit
+            split = (SPLIT_HEAD if q < HEAD_PAIRS else SPLIT) * n // CHUNK
+            t = stage.tile([P, CHUNK, PACK], BF16, name="grouped", align_bytes=64)
+            grouped[unit] = t
+            raw = x_raw[unit]
+            nc.scalar.copy(
+                out=runs4(t[:, 0:split, :], "p (c i) t -> p c t i"),
+                in_=runs4(raw[:, :, 0:split], "p t (c i) -> p c t i"),
+            )
+            nc.vector.tensor_copy(
+                out=runs4(t[:, split:n, :], "p (c i) t -> p c t i"),
+                in_=runs4(raw[:, :, split:n], "p t (c i) -> p c t i"),
+            )
+
+        def x_quant(unit):
+            q, g, c0, n = unit
+            nc.vector.quantize_mx(
+                out=x_codes[:, q, g, c0 : c0 + n].bitcast(FP8X4),
+                scales=x_scales[:, q, g, c0 : c0 + n],
+                in_=grouped[unit][:, 0:n, :].rearrange("p w j -> p (w j)"),
+            )
+
+        def pair_copy(q):
+            t = stage.tile([P, G, CHUNK, PACK], BF16, name="grouped2", align_bytes=64)
+            grouped[q] = t
+            raw = x_raw[q][:]
+            for g in range(G):
+                nc.scalar.copy(
+                    out=runs4(t[:, g, 0:SPLIT, :], "p (c i) t -> p c t i"),
+                    in_=runs4(raw[:, g, :, 0:SPLIT], "p t (c i) -> p c t i"),
+                )
+            nc.vector.tensor_copy(
+                out=runs4(t[:, :, SPLIT:CHUNK, :], "p g (c i) t -> p g c t i"),
+                in_=runs4(raw[:, :, :, SPLIT:CHUNK], "p g t (c i) -> p g c t i"),
+            )
+
+        def pair_quant(q):
+            nc.vector.quantize_mx(
+                out=x_codes[:, q, :, :].rearrange("p g c -> p (g c)").bitcast(FP8X4),
+                scales=x_scales[:, q, :, :].rearrange("p g c -> p (g c)"),
+                in_=grouped[q][:].rearrange("p g w j -> p (g w j)"),
+            )
+
+        SHIFT = {4: (-LINE, 0), 0: (0, 0), 3: (LINE, 0), 1: (0, -1), 2: (0, 1)}
+
+        def side(q, g, c0=0, n=CHUNK):
+            return [((q, 0), c0, n, 6, g, (q, c0)), ((q, 1), c0, n, 5, g, (q, c0))]
+
+        def centre(q, h, g, ks):
+            s = 2 * q + h
+            found = []
+            for k in ks:
+                shift, d = SHIFT[k]
+                if not 0 <= s % 8 + d <= 7:
+                    continue
+                found.append(((q, 2 + h), BASE + shift, SLICE, k, g, ((s + d) // 2, SLICE * ((s + d) % 2))))
+                if k == 4 and g == 0:
+                    found.append(((q, 2 + h), SLICE, P, k, g, None))
+            return found
+
+        plan = []
+        for q in range(N_PAIRS):
+            seg = []
+            if q == 0:
+                plan.append(side(q, 0, 0, SLICE) + centre(q, 0, 0, (4, 0, 3)))
+                plan.append(side(q, 0, SLICE, SLICE) + centre(q, 1, 0, (4, 0, 3, 1)) + centre(q, 0, 0, (2,)))
+                seg += side(q, 1) + centre(q, 0, 1, (4, 0, 3, 2)) + centre(q, 1, 1, (4, 0, 3, 1))
+            elif q == 1:
+                for g in range(G):
+                    seg += centre(q - 1, 1, g, (2,)) + side(q, g)
+                    seg += centre(q, 0, g, (4, 0, 3, 1, 2)) + centre(q, 1, g, (4, 0, 3, 1))
+            else:
+                for g in range(G):
+                    seg += centre(q - 1, 1, g, (2,))
+                for g in range(G):
+                    seg += side(q, g)
+                for h in range(2):
+                    for k in (4, 0, 3, 1, 2) if h == 0 else (4, 0, 3, 1):
+                        for g in range(G):
+                            seg += centre(q, h, g, (k,))
+            plan.append(seg)
+        flat = [item[0] for seg in plan for item in seg]
+        first = {}
+        last = {}
+        for i, key in enumerate(flat):
+            if key not in first:
+                first[key] = i
+            last[key] = i
+        banks = {}
+        count = [0]
+
+        def passes(part):
+            for key, lo, n, k, g, xat in plan[part]:
+                if key not in banks:
+                    banks[key] = bank(4 * (key[0] % 2) + key[1], "acc%d" % key[1])
+                if xat is None:
+                    rhs, rhs_scale = zero_codes[:], zero_scales[:]
+                else:
+                    rhs = x_codes[:, xat[0], g, xat[1] : xat[1] + n]
+                    rhs_scale = x_scales[:, xat[0], g, xat[1] : xat[1] + n]
+                i = count[0]
+                count[0] = i + 1
+                nc.tensor.matmul_mx(
+                    out=banks[key][:, lo : lo + n],
+                    lhsT=w_codes[:, k, P * g : P * (g + 1)].bitcast(FP8X4),
+                    lhsT_scale=w_scales[:, k, P * g : P * (g + 1)],
+                    rhs=rhs.bitcast(FP8X4),
+                    rhs_scale=rhs_scale,
+                    start=(first[key] == i),
+                    stop=(last[key] == i),
+                )
+
+        def main_copy(q, h):
+            nc.scalar.copy(
+                out=res[:, q, SLICE * h : SLICE * (h + 1)], in_=banks[(q, 2 + h)][:, BASE : BASE + SLICE]
+            )
+
+        def main_add(q, h):
+            cols = slice(SLICE * h, SLICE * (h + 1))
+            nc.vector.tensor_tensor(
+                out=res[:, q, cols], in0=res[:, q, cols], in1=banks[(q, 2 + h)][:, BASE : BASE + SLICE], op=ADD
+            )
+
+        def side_copy(q):
+            nc.scalar.copy(
+                out=lines(res[:, q, :])[:, :, 0 : LINE - 1], in_=lines(banks[(q, 0)][:])[:, :, 1:LINE]
+            )
+
+        def side_add(q, which):
+            r3 = lines(res[:, q, :])
+            y3 = lines(banks[(q, which)][:])
+            if which == 1:
+                dst, src = r3[:, :, 1:LINE], y3[:, :, 0 : LINE - 1]
+            else:
+                dst, src = r3[:, :, 0 : LINE - 1], y3[:, :, 1:LINE]
+            nc.vector.tensor_tensor(out=dst, in0=dst, in1=src, op=ADD)
+
+        def store(q, lo, n):
+            b, qq = divmod(q, 4)
+            ob = out[b].rearrange("o t r c -> o (t r c)")
+            nc.sync.dma_start(out=ob[:, CHUNK * qq + lo : CHUNK * qq + lo + n], in_=res[:, q, lo : lo + n])
+
+        def prepare(q):
+            if q >= N_PAIRS:
+                return
+            if q < FINE_PAIRS:
+                for g in range(G):
+                    x_copy((q, g, 0, CHUNK))
+                    x_quant((q, g, 0, CHUNK))
+            else:
+                pair_copy(q)
+                pair_quant(q)
+
+        def w_prepare(i, k):
+            w_copy(i, k)
+            w_quant(k)
+
+        for i, k in enumerate(W_FIRST):
+            w_transposes(i, k)
+        for i, k in enumerate(W_LATER):
+            w_transposes(5 + i, k)
+        for i, k in enumerate(W_FIRST):
+            w_prepare(i, k)
+        early = HEAD_UNITS + [(q, g, 0, CHUNK) for q in range(1, FINE_PAIRS) for g in range(G)]
+        x_copy(early[0])
+        x_quant(early[0])
+        passes(0)
+        x_copy(early[1])
+        for i, k in enumerate(W_LATER):
+            w_prepare(5 + i, k)
+        for j in range(1, len(early)):
+            if j + 1 < len(early):
+                x_copy(early[j + 1])
+            x_quant(early[j])
+            if j == 1:
+                passes(1)
+        LAST = N_PAIRS - 1
+        for q in range(N_PAIRS):
+            passes(q + 2)
+            if q >= 1:
+                main_copy(q - 1, 1)
+                side_add(q - 1, 0)
+                side_add(q - 1, 1)
+                store(q - 1, 0, CHUNK)
+            if q == LAST:
+                break
+            if q + 2 >= FINE_PAIRS:
+                prepare(q + 2)
+            main_copy(q, 0)
+        side_copy(LAST)
+        side_add(LAST, 1)
+        main_add(LAST, 0)
+        store(LAST, 0, SLICE)
+        main_add(LAST, 1)
+        store(LAST, SLICE, SLICE)

@@ -24,19 +24,16 @@ SPLIT_HEAD = 256
 SPLIT = 320
 W_FIRST = (6, 5, 4, 0, 3)
 W_LATER = (2, 1)
-PINNED = True
-HEAD_PAIRS = 3
 FINE_PAIRS = 3
-W_ON_VECTOR = 0
-HEAD_UNITS = [(0, 0, 0, SLICE), (0, 0, SLICE, SLICE), (0, 1, 0, CHUNK)]
+HEAD_UNITS = [(0, g, SLICE * h, SLICE) for g in range(G) for h in range(2)]
+S_SHARE = {HEAD_UNITS[0]: 0, HEAD_UNITS[1]: 0, HEAD_UNITS[2]: SLICE, HEAD_UNITS[3]: 0}
 UNITS = [(q, g, 0, CHUNK) for q in range(1, N_PAIRS) for g in range(G)]
 
 
 def tile_stackeddirectionalconv3d_t_kernel(tc, x, W, out):
     nc = tc.nc
     with ExitStack() as ctx:
-        if PINNED:
-            ctx.enter_context(tc.manual_schedule())
+        ctx.enter_context(tc.manual_schedule())
         keep = ctx.enter_context(tc.tile_pool(name="keep", bufs=1))
         stage = ctx.enter_context(tc.tile_pool(name="stage", bufs=3))
         psum = ctx.enter_context(tc.psum_pool(name="psum", bufs=1))
@@ -105,13 +102,10 @@ def tile_stackeddirectionalconv3d_t_kernel(tc, x, W, out):
         w_grouped = {}
 
         def w_copy(i, k):
-            w_grouped[k] = stage.tile([P, G * P * PACK], BF16, name="w_grouped", align_bytes=64)
+            w_grouped[k] = keep.tile([P, G * P * PACK], BF16, name="w_grouped%d" % k, align_bytes=64)
             dst = w_grouped[k][:].bitcast(F32).rearrange("p (g o u) -> p g o u", g=G, u=2)
             src = wt[k][:].rearrange("p (g u o) -> p g o u", g=G, u=2)
-            if W_ON_VECTOR and i % W_ON_VECTOR == W_ON_VECTOR - 1:
-                nc.vector.tensor_copy(out=dst, in_=src)
-            else:
-                nc.scalar.copy(out=dst, in_=src)
+            nc.scalar.copy(out=dst, in_=src)
 
         def w_quant(k):
             nc.vector.quantize_mx(
@@ -125,18 +119,20 @@ def tile_stackeddirectionalconv3d_t_kernel(tc, x, W, out):
 
         def x_copy(unit):
             q, g, c0, n = unit
-            split = (SPLIT_HEAD if q < HEAD_PAIRS else SPLIT) * n // CHUNK
+            split = S_SHARE.get(unit, SPLIT_HEAD)
             t = stage.tile([P, CHUNK, PACK], BF16, name="grouped", align_bytes=64)
             grouped[unit] = t
             raw = x_raw[unit]
-            nc.scalar.copy(
-                out=runs4(t[:, 0:split, :], "p (c i) t -> p c t i"),
-                in_=runs4(raw[:, :, 0:split], "p t (c i) -> p c t i"),
-            )
-            nc.vector.tensor_copy(
-                out=runs4(t[:, split:n, :], "p (c i) t -> p c t i"),
-                in_=runs4(raw[:, :, split:n], "p t (c i) -> p c t i"),
-            )
+            if split > 0:
+                nc.scalar.copy(
+                    out=runs4(t[:, 0:split, :], "p (c i) t -> p c t i"),
+                    in_=runs4(raw[:, :, 0:split], "p t (c i) -> p c t i"),
+                )
+            if split < n:
+                nc.vector.tensor_copy(
+                    out=runs4(t[:, split:n, :], "p (c i) t -> p c t i"),
+                    in_=runs4(raw[:, :, split:n], "p t (c i) -> p c t i"),
+                )
 
         def x_quant(unit):
             q, g, c0, n = unit
@@ -190,7 +186,8 @@ def tile_stackeddirectionalconv3d_t_kernel(tc, x, W, out):
             if q == 0:
                 plan.append(side(q, 0, 0, SLICE) + centre(q, 0, 0, (4, 0, 3)))
                 plan.append(side(q, 0, SLICE, SLICE) + centre(q, 1, 0, (4, 0, 3, 1)) + centre(q, 0, 0, (2,)))
-                seg += side(q, 1) + centre(q, 0, 1, (4, 0, 3, 2)) + centre(q, 1, 1, (4, 0, 3, 1))
+                plan.append(side(q, 1, 0, SLICE) + centre(q, 0, 1, (4, 0, 3)))
+                seg += side(q, 1, SLICE, SLICE) + centre(q, 1, 1, (4, 0, 3, 1)) + centre(q, 0, 1, (2,))
             elif q == 1:
                 for g in range(G):
                     seg += centre(q - 1, 1, g, (2,)) + side(q, g)
@@ -277,32 +274,37 @@ def tile_stackeddirectionalconv3d_t_kernel(tc, x, W, out):
                 pair_copy(q)
                 pair_quant(q)
 
-        def w_prepare(i, k):
-            w_copy(i, k)
-            w_quant(k)
-
         for i, k in enumerate(W_FIRST):
             w_transposes(i, k)
         for i, k in enumerate(W_LATER):
             w_transposes(5 + i, k)
-        for i, k in enumerate(W_FIRST):
-            w_prepare(i, k)
-        early = HEAD_UNITS + [(q, g, 0, CHUNK) for q in range(1, FINE_PAIRS) for g in range(G)]
-        x_copy(early[0])
-        x_quant(early[0])
+        for i, k in enumerate(W_FIRST + W_LATER):
+            w_copy(i, k)
+        head = HEAD_UNITS
+        for k in W_FIRST[:3]:
+            w_quant(k)
+        x_copy(head[0])
+        w_quant(W_FIRST[3])
+        x_quant(head[0])
+        w_quant(W_FIRST[4])
         passes(0)
-        x_copy(early[1])
-        for i, k in enumerate(W_LATER):
-            w_prepare(5 + i, k)
-        for j in range(1, len(early)):
+        x_copy(head[1])
+        w_quant(W_LATER[0])
+        x_quant(head[1])
+        w_quant(W_LATER[1])
+        passes(1)
+        x_copy(head[2])
+        x_copy(head[3])
+        x_quant(head[2])
+        passes(2)
+        early = head[3:] + [(q, g, 0, CHUNK) for q in range(1, FINE_PAIRS) for g in range(G)]
+        for j in range(len(early)):
             if j + 1 < len(early):
                 x_copy(early[j + 1])
             x_quant(early[j])
-            if j == 1:
-                passes(1)
         LAST = N_PAIRS - 1
         for q in range(N_PAIRS):
-            passes(q + 2)
+            passes(q + 3)
             if q >= 1:
                 main_copy(q - 1, 1)
                 side_add(q - 1, 0)

@@ -20,14 +20,72 @@ CHUNK = 512
 N_PAIRS = 8
 LINE = 16
 BASE = 16
-SPLIT_HEAD = 256
-SPLIT = 320
-W_FIRST = (6, 5, 4, 0, 3)
-W_LATER = (2, 1)
-FINE_PAIRS = 3
-HEAD_UNITS = [(0, g, SLICE * h, SLICE) for g in range(G) for h in range(2)]
-S_SHARE = {HEAD_UNITS[0]: 0, HEAD_UNITS[1]: 0, HEAD_UNITS[2]: SLICE, HEAD_UNITS[3]: 0}
-UNITS = [(q, g, 0, CHUNK) for q in range(1, N_PAIRS) for g in range(G)]
+SPLIT = 256
+WIDE_FROM = 3
+LOADS = [6, 5, 4, 0, 3, (0, 0, 1), 2, 1, (0, 1, 1), (1, 0, 1), (1, 1, 1), (2, 0, 1), (2, 1, 1), (3, 0, 1), (3, 1, 1), (4, 0, 2), (4, 1, 2), (6, 0, 2), (6, 1, 2)]
+HEAD = [
+    ("wt", 6, 0),
+    ("wt", 5, 1),
+    ("wt", 4, 2),
+    ("wt", 0, 3),
+    ("wt", 3, 4),
+    ("wt", 2, 5),
+    ("wt", 1, 6),
+    ("wc", 6),
+    ("wc", 5),
+    ("wc", 4),
+    ("wc", 0),
+    ("wc", 3),
+    ("wq", 6),
+    ("wq", 5),
+    ("wq", 4),
+    ("wq", 0),
+    ("xc", 0, 0, 0, 256, 0),
+    ("wq", 3),
+    ("xq", 0, 0, 0, 256),
+    ("side", 0, 6, 0, 0, 256),
+    ("side", 0, 5, 0, 0, 256),
+    ("main", 0, 0, 4, 0),
+    ("main", 0, 0, 0, 0),
+    ("main", 0, 0, 3, 0),
+    ("xc", 0, 0, 256, 256, 256),
+    ("wc", 2),
+    ("wc", 1),
+    ("xq", 0, 0, 256, 256),
+    ("side", 0, 6, 0, 256, 256),
+    ("side", 0, 5, 0, 256, 256),
+    ("main", 0, 1, 4, 0),
+    ("main", 0, 1, 0, 0),
+    ("main", 0, 1, 3, 0),
+    ("wq", 2),
+    ("main", 0, 0, 2, 0),
+    ("xc", 0, 1, 0, 256, 0),
+    ("xc", 0, 1, 256, 256, 256),
+    ("xq", 0, 1, 0, 256),
+    ("side", 0, 6, 1, 0, 256),
+    ("side", 0, 5, 1, 0, 256),
+    ("main", 0, 0, 4, 1),
+    ("main", 0, 0, 0, 1),
+    ("main", 0, 0, 3, 1),
+    ("wq", 1),
+    ("main", 0, 1, 1, 0),
+    ("xc", 1, 0, 0, 512, 256),
+    ("xq", 0, 1, 256, 256),
+    ("side", 0, 6, 1, 256, 256),
+    ("side", 0, 5, 1, 256, 256),
+    ("main", 0, 1, 4, 1),
+    ("main", 0, 1, 0, 1),
+    ("main", 0, 1, 3, 1),
+    ("main", 0, 0, 2, 1),
+    ("main", 0, 1, 1, 1),
+    ("xc", 1, 1, 0, 512, 256),
+    ("xq", 1, 0, 0, 512),
+    ("xc", 2, 0, 0, 512, 256),
+    ("xq", 1, 1, 0, 512),
+    ("xc", 2, 1, 0, 512, 256),
+    ("xq", 2, 0, 0, 512),
+    ("xq", 2, 1, 0, 512),
+]
 
 
 def tile_stackeddirectionalconv3d_t_kernel(tc, x, W, out):
@@ -38,10 +96,10 @@ def tile_stackeddirectionalconv3d_t_kernel(tc, x, W, out):
         stage = ctx.enter_context(tc.tile_pool(name="stage", bufs=3))
         psum = ctx.enter_context(tc.psum_pool(name="psum", bufs=1))
 
-        x_codes = keep.tile([P, N_PAIRS, G, CHUNK], U32, name="x_codes", align_bytes=64)
-        x_scales = keep.tile([P, N_PAIRS, G, CHUNK], U8, name="x_scales", align_bytes=64)
-        w_codes = keep.tile([P, 7, G * P], U32, name="w_codes", align_bytes=64)
-        w_scales = keep.tile([P, 7, G * P], U8, name="w_scales", align_bytes=64)
+        x_codes = keep.tile([P, N_PAIRS, G, CHUNK], U32, name="x_codes", align_bytes=256)
+        x_scales = keep.tile([P, N_PAIRS, G, CHUNK], U8, name="x_scales", align_bytes=256)
+        w_codes = keep.tile([P, 7, G * P], U32, name="w_codes", align_bytes=256)
+        w_scales = keep.tile([P, 7, G * P], U8, name="w_scales", align_bytes=256)
         zero_bf = keep.tile([P, P * PACK], BF16, name="zero_bf", align_bytes=64)
         zero_codes = keep.tile([P, P], U32, name="zero_codes", align_bytes=64)
         zero_scales = keep.tile([P, P], U8, name="zero_scales", align_bytes=64)
@@ -49,48 +107,50 @@ def tile_stackeddirectionalconv3d_t_kernel(tc, x, W, out):
         res = keep.tile([P, N_PAIRS, CHUNK], F32, name="res")
 
         w_raw = {}
+        x_raw = {}
+        wide = {}
 
         def load_w(k):
             w_raw[k] = keep.tile([P, 1024], BF16, name="w_raw%d" % k)
             nc.sync.dma_start(out=w_raw[k][:], in_=W[P * k : P * (k + 1), :])
 
-        x_raw = {}
+        x_tiles = {}
 
-        def load_x(unit):
-            q, g, c0, n = unit
-            if q < FINE_PAIRS:
-                x_raw[unit] = keep.tile([P, PACK, n], BF16, name="x_raw_%d_%d_%d" % (q, g, c0))[:]
-            else:
-                if g == 0:
-                    x_raw[q] = keep.tile([P, G, PACK, CHUNK], BF16, name="x_raw_%d" % q)
-                x_raw[unit] = x_raw[q][:, g, :, :]
+        def load_x(q, g, m, c0=0, n=CHUNK):
+            if (q, m) not in x_tiles:
+                x_tiles[(q, m)] = keep.tile([P, G, PACK, m * CHUNK], BF16, name="x_raw_%d" % q)
+            t = x_tiles[(q, m)]
+            for i in range(m):
+                x_raw[(q + i, g)] = t[:, g, :, CHUNK * i : CHUNK * (i + 1)]
+                wide[q + i] = t[:, :, :, CHUNK * i : CHUNK * (i + 1)]
             b, qq = divmod(q, 4)
             xb = x[b].rearrange("k t r c -> k (t r c)")
-            rows = xb[512 * g : 512 * g + 512, CHUNK * qq + c0 : CHUNK * qq + c0 + n]
-            nc.sync.dma_start(out=x_raw[unit], in_=rows.rearrange("(p e) w -> p e w", e=PACK))
+            width = m * CHUNK if m > 1 else n
+            rows = xb[512 * g : 512 * g + 512, CHUNK * qq + c0 : CHUNK * qq + c0 + width]
+            nc.sync.dma_start(
+                out=t[:, g, :, c0 : c0 + width], in_=rows.rearrange("(p e) w -> p e w", e=PACK)
+            )
 
-        for k in W_FIRST:
-            load_w(k)
-        load_x(HEAD_UNITS[0])
-        for k in W_LATER:
-            load_w(k)
-        for unit in HEAD_UNITS[1:] + UNITS:
-            load_x(unit)
+        for item in LOADS:
+            if isinstance(item, int):
+                load_w(item)
+            else:
+                load_x(*item)
 
         def lines(ap):
             return ap.rearrange("p (l c) -> p l c", c=LINE)
 
         make_identity(nc, ident[:])
         nc.vector.memset(zero_bf[:], 0.0)
-        nc.vector.memset(lines(res[:, N_PAIRS - 1, :])[:, :, LINE - 1 : LINE], 0.0)
         nc.vector.quantize_mx(out=zero_codes[:].bitcast(FP8X4), scales=zero_scales[:], in_=zero_bf[:])
+        nc.gpsimd.memset(res[:].rearrange("p q (l c) -> p (q l) c", c=LINE)[:, :, LINE - 1 : LINE], 0.0)
 
         def bank(i, name):
             return psum.tile([P, 512], F32, name=name, tag="bank%d" % i)
 
         wt = {}
 
-        def w_transposes(i, k):
+        def wt_(k, i):
             words = w_raw[k][:].bitcast(F32)
             wt[k] = bank(i, "wt%d" % k)
             for j in range(4):
@@ -101,13 +161,16 @@ def tile_stackeddirectionalconv3d_t_kernel(tc, x, W, out):
 
         w_grouped = {}
 
-        def w_copy(i, k):
+        def wc_(k, e="s"):
             w_grouped[k] = keep.tile([P, G * P * PACK], BF16, name="w_grouped%d" % k, align_bytes=64)
             dst = w_grouped[k][:].bitcast(F32).rearrange("p (g o u) -> p g o u", g=G, u=2)
             src = wt[k][:].rearrange("p (g u o) -> p g o u", g=G, u=2)
-            nc.scalar.copy(out=dst, in_=src)
+            if e == "s":
+                nc.scalar.copy(out=dst, in_=src)
+            else:
+                nc.vector.tensor_copy(out=dst, in_=src)
 
-        def w_quant(k):
+        def wq_(k):
             nc.vector.quantize_mx(
                 out=w_codes[:, k, :].bitcast(FP8X4), scales=w_scales[:, k, :], in_=w_grouped[k][:]
             )
@@ -117,46 +180,45 @@ def tile_stackeddirectionalconv3d_t_kernel(tc, x, W, out):
         def runs4(ap, order):
             return ap.rearrange(order, i=4)
 
-        def x_copy(unit):
-            q, g, c0, n = unit
-            split = S_SHARE.get(unit, SPLIT_HEAD)
+        def xc_(q, g, c0, n, s):
             t = stage.tile([P, CHUNK, PACK], BF16, name="grouped", align_bytes=64)
-            grouped[unit] = t
-            raw = x_raw[unit]
-            if split > 0:
+            grouped[(q, g, c0)] = t
+            raw = x_raw[(q, g)]
+            if s > 0:
                 nc.scalar.copy(
-                    out=runs4(t[:, 0:split, :], "p (c i) t -> p c t i"),
-                    in_=runs4(raw[:, :, 0:split], "p t (c i) -> p c t i"),
+                    out=runs4(t[:, 0:s, :], "p (c i) t -> p c t i"),
+                    in_=runs4(raw[:, :, c0 : c0 + s], "p t (c i) -> p c t i"),
                 )
-            if split < n:
+            if s < n:
                 nc.vector.tensor_copy(
-                    out=runs4(t[:, split:n, :], "p (c i) t -> p c t i"),
-                    in_=runs4(raw[:, :, split:n], "p t (c i) -> p c t i"),
+                    out=runs4(t[:, s:n, :], "p (c i) t -> p c t i"),
+                    in_=runs4(raw[:, :, c0 + s : c0 + n], "p t (c i) -> p c t i"),
                 )
 
-        def x_quant(unit):
-            q, g, c0, n = unit
+        def xq_(q, g, c0, n):
             nc.vector.quantize_mx(
                 out=x_codes[:, q, g, c0 : c0 + n].bitcast(FP8X4),
                 scales=x_scales[:, q, g, c0 : c0 + n],
-                in_=grouped[unit][:, 0:n, :].rearrange("p w j -> p (w j)"),
+                in_=grouped[(q, g, c0)][:, 0:n, :].rearrange("p w j -> p (w j)"),
             )
 
-        def pair_copy(q):
-            t = stage.tile([P, G, CHUNK, PACK], BF16, name="grouped2", align_bytes=64)
-            grouped[q] = t
-            raw = x_raw[q][:]
+        def pair_tile(q):
+            grouped[q] = stage.tile([P, G, CHUNK, PACK], BF16, name="grouped2", align_bytes=64)
+
+        def pair_s(q, g):
+            nc.scalar.copy(
+                out=runs4(grouped[q][:, g, 0:SPLIT, :], "p (c i) t -> p c t i"),
+                in_=runs4(wide[q][:, g, :, 0:SPLIT], "p t (c i) -> p c t i"),
+            )
+
+        def pair_v(q):
             for g in range(G):
-                nc.scalar.copy(
-                    out=runs4(t[:, g, 0:SPLIT, :], "p (c i) t -> p c t i"),
-                    in_=runs4(raw[:, g, :, 0:SPLIT], "p t (c i) -> p c t i"),
+                nc.vector.tensor_copy(
+                    out=runs4(grouped[q][:, g, SPLIT:CHUNK, :], "p (c i) t -> p c t i"),
+                    in_=runs4(wide[q][:, g, :, SPLIT:CHUNK], "p t (c i) -> p c t i"),
                 )
-            nc.vector.tensor_copy(
-                out=runs4(t[:, :, SPLIT:CHUNK, :], "p g (c i) t -> p g c t i"),
-                in_=runs4(raw[:, :, :, SPLIT:CHUNK], "p g t (c i) -> p g c t i"),
-            )
 
-        def pair_quant(q):
+        def pair_q(q):
             nc.vector.quantize_mx(
                 out=x_codes[:, q, :, :].rearrange("p g c -> p (g c)").bitcast(FP8X4),
                 scales=x_scales[:, q, :, :].rearrange("p g c -> p (g c)"),
@@ -164,79 +226,56 @@ def tile_stackeddirectionalconv3d_t_kernel(tc, x, W, out):
             )
 
         SHIFT = {4: (-LINE, 0), 0: (0, 0), 3: (LINE, 0), 1: (0, -1), 2: (0, 1)}
-
-        def side(q, g, c0=0, n=CHUNK):
-            return [((q, 0), c0, n, 6, g, (q, c0)), ((q, 1), c0, n, 5, g, (q, c0))]
-
-        def centre(q, h, g, ks):
-            s = 2 * q + h
-            found = []
-            for k in ks:
-                shift, d = SHIFT[k]
-                if not 0 <= s % 8 + d <= 7:
-                    continue
-                found.append(((q, 2 + h), BASE + shift, SLICE, k, g, ((s + d) // 2, SLICE * ((s + d) % 2))))
-                if k == 4 and g == 0:
-                    found.append(((q, 2 + h), SLICE, P, k, g, None))
-            return found
-
-        plan = []
-        for q in range(N_PAIRS):
-            seg = []
-            if q == 0:
-                plan.append(side(q, 0, 0, SLICE) + centre(q, 0, 0, (4, 0, 3)))
-                plan.append(side(q, 0, SLICE, SLICE) + centre(q, 1, 0, (4, 0, 3, 1)) + centre(q, 0, 0, (2,)))
-                plan.append(side(q, 1, 0, SLICE) + centre(q, 0, 1, (4, 0, 3)))
-                seg += side(q, 1, SLICE, SLICE) + centre(q, 1, 1, (4, 0, 3, 1)) + centre(q, 0, 1, (2,))
-            elif q == 1:
-                for g in range(G):
-                    seg += centre(q - 1, 1, g, (2,)) + side(q, g)
-                    seg += centre(q, 0, g, (4, 0, 3, 1, 2)) + centre(q, 1, g, (4, 0, 3, 1))
-            else:
-                for g in range(G):
-                    seg += centre(q - 1, 1, g, (2,))
-                for g in range(G):
-                    seg += side(q, g)
-                for h in range(2):
-                    for k in (4, 0, 3, 1, 2) if h == 0 else (4, 0, 3, 1):
-                        for g in range(G):
-                            seg += centre(q, h, g, (k,))
-            plan.append(seg)
-        flat = [item[0] for seg in plan for item in seg]
-        first = {}
-        last = {}
-        for i, key in enumerate(flat):
-            if key not in first:
-                first[key] = i
-            last[key] = i
         banks = {}
-        count = [0]
+        done = {}
 
-        def passes(part):
-            for key, lo, n, k, g, xat in plan[part]:
-                if key not in banks:
-                    banks[key] = bank(4 * (key[0] % 2) + key[1], "acc%d" % key[1])
-                if xat is None:
-                    rhs, rhs_scale = zero_codes[:], zero_scales[:]
-                else:
-                    rhs = x_codes[:, xat[0], g, xat[1] : xat[1] + n]
-                    rhs_scale = x_scales[:, xat[0], g, xat[1] : xat[1] + n]
-                i = count[0]
-                count[0] = i + 1
-                nc.tensor.matmul_mx(
-                    out=banks[key][:, lo : lo + n],
-                    lhsT=w_codes[:, k, P * g : P * (g + 1)].bitcast(FP8X4),
-                    lhsT_scale=w_scales[:, k, P * g : P * (g + 1)],
-                    rhs=rhs.bitcast(FP8X4),
-                    rhs_scale=rhs_scale,
-                    start=(first[key] == i),
-                    stop=(last[key] == i),
-                )
+        def valid(s, k):
+            return 0 <= s % 8 + SHIFT[k][1] <= 7
 
-        def main_copy(q, h):
-            nc.scalar.copy(
-                out=res[:, q, SLICE * h : SLICE * (h + 1)], in_=banks[(q, 2 + h)][:, BASE : BASE + SLICE]
+        def mx(key, lo, n, k, g, rhs, rhs_scale, total):
+            if key not in banks:
+                banks[key] = bank(4 * (key[0] % 2) + key[1], "acc%d" % key[1])
+            i = done.get(key, 0)
+            done[key] = i + n
+            nc.tensor.matmul_mx(
+                out=banks[key][:, lo : lo + n],
+                lhsT=w_codes[:, k, P * g : P * (g + 1)].bitcast(FP8X4),
+                lhsT_scale=w_scales[:, k, P * g : P * (g + 1)],
+                rhs=rhs.bitcast(FP8X4),
+                rhs_scale=rhs_scale,
+                start=(i == 0),
+                stop=(i + n == total),
             )
+
+        def x_cols(q, g, c0, n):
+            return x_codes[:, q, g, c0 : c0 + n], x_scales[:, q, g, c0 : c0 + n]
+
+        def side(q, k, g, c0=0, n=CHUNK):
+            mx((q, 0 if k == 6 else 1), c0, n, k, g, *x_cols(q, g, c0, n), G * CHUNK)
+
+        def main(q, h, k, g):
+            s = 2 * q + h
+            if not valid(s, k):
+                return
+            total = P + SLICE * G * sum(valid(s, j) for j in SHIFT)
+            shift, d = SHIFT[k]
+            xs = s + d
+            key = (q, 2 + h)
+            mx(key, BASE + shift, SLICE, k, g, *x_cols(xs // 2, g, SLICE * (xs % 2), SLICE), total)
+            if k == 4 and key not in marked:
+                marked.add(key)
+                mx(key, SLICE, P, k, g, zero_codes[:], zero_scales[:], total)
+
+        marked = set()
+
+        def side_copy(q):
+            nc.scalar.copy(
+                out=lines(res[:, q, :])[:, :, 0 : LINE - 1], in_=lines(banks[(q, 0)][:])[:, :, 1:LINE]
+            )
+
+        def side_add(q):
+            dst = lines(res[:, q, :])[:, :, 1:LINE]
+            nc.vector.tensor_tensor(out=dst, in0=dst, in1=lines(banks[(q, 1)][:])[:, :, 0 : LINE - 1], op=ADD)
 
         def main_add(q, h):
             cols = slice(SLICE * h, SLICE * (h + 1))
@@ -244,80 +283,64 @@ def tile_stackeddirectionalconv3d_t_kernel(tc, x, W, out):
                 out=res[:, q, cols], in0=res[:, q, cols], in1=banks[(q, 2 + h)][:, BASE : BASE + SLICE], op=ADD
             )
 
-        def side_copy(q):
-            nc.scalar.copy(
-                out=lines(res[:, q, :])[:, :, 0 : LINE - 1], in_=lines(banks[(q, 0)][:])[:, :, 1:LINE]
-            )
-
-        def side_add(q, which):
-            r3 = lines(res[:, q, :])
-            y3 = lines(banks[(q, which)][:])
-            if which == 1:
-                dst, src = r3[:, :, 1:LINE], y3[:, :, 0 : LINE - 1]
-            else:
-                dst, src = r3[:, :, 0 : LINE - 1], y3[:, :, 1:LINE]
-            nc.vector.tensor_tensor(out=dst, in0=dst, in1=src, op=ADD)
-
         def store(q, lo, n):
             b, qq = divmod(q, 4)
             ob = out[b].rearrange("o t r c -> o (t r c)")
             nc.sync.dma_start(out=ob[:, CHUNK * qq + lo : CHUNK * qq + lo + n], in_=res[:, q, lo : lo + n])
 
-        def prepare(q):
-            if q >= N_PAIRS:
-                return
-            if q < FINE_PAIRS:
-                for g in range(G):
-                    x_copy((q, g, 0, CHUNK))
-                    x_quant((q, g, 0, CHUNK))
-            else:
-                pair_copy(q)
-                pair_quant(q)
+        acts = {"wt": wt_, "wc": wc_, "wq": wq_, "xc": xc_, "xq": xq_, "side": side, "main": main}
+        for step in HEAD:
+            acts[step[0]](*step[1:])
 
-        for i, k in enumerate(W_FIRST):
-            w_transposes(i, k)
-        for i, k in enumerate(W_LATER):
-            w_transposes(5 + i, k)
-        for i, k in enumerate(W_FIRST + W_LATER):
-            w_copy(i, k)
-        head = HEAD_UNITS
-        for k in W_FIRST[:3]:
-            w_quant(k)
-        x_copy(head[0])
-        w_quant(W_FIRST[3])
-        x_quant(head[0])
-        w_quant(W_FIRST[4])
-        passes(0)
-        x_copy(head[1])
-        w_quant(W_LATER[0])
-        x_quant(head[1])
-        w_quant(W_LATER[1])
-        passes(1)
-        x_copy(head[2])
-        x_copy(head[3])
-        x_quant(head[2])
-        passes(2)
-        early = head[3:] + [(q, g, 0, CHUNK) for q in range(1, FINE_PAIRS) for g in range(G)]
-        for j in range(len(early)):
-            if j + 1 < len(early):
-                x_copy(early[j + 1])
-            x_quant(early[j])
         LAST = N_PAIRS - 1
+        FINE = 2
+
+        def tail_of(q):
+            for g in range(G):
+                main(q, 1, 2, g)
+
+        def body(q):
+            for g in range(G):
+                for k in (6, 5):
+                    side(q, k, g)
+            for h in range(2):
+                for k in (4, 0, 3, 1, 2) if h == 0 else (4, 0, 3, 1):
+                    for g in range(G):
+                        main(q, h, k, g)
+
+        def body_fine(q):
+            for g in range(G):
+                main(q - 1, 1, 2, g)
+                for k in (6, 5):
+                    side(q, k, g)
+                for h in range(2):
+                    for k in (4, 0, 3, 1, 2) if h == 0 else (4, 0, 3, 1):
+                        main(q, h, k, g)
+
         for q in range(N_PAIRS):
-            passes(q + 3)
+            ahead = q + 2
+            prep = WIDE_FROM <= ahead < N_PAIRS
             if q >= 1:
-                main_copy(q - 1, 1)
-                side_add(q - 1, 0)
-                side_add(q - 1, 1)
+                if q < FINE:
+                    body_fine(q)
+                else:
+                    tail_of(q - 1)
+                    body(q)
+            if prep:
+                pair_tile(ahead)
+                pair_s(ahead, 0)
+            side_copy(q)
+            if prep:
+                pair_s(ahead, 1)
+            if q >= 1:
+                main_add(q - 1, 1)
                 store(q - 1, 0, CHUNK)
-            if q == LAST:
-                break
-            if q + 2 >= FINE_PAIRS:
-                prepare(q + 2)
-            main_copy(q, 0)
-        side_copy(LAST)
-        side_add(LAST, 1)
-        main_add(LAST, 0)
+            if prep:
+                pair_v(ahead)
+            side_add(q)
+            if prep:
+                pair_q(ahead)
+            main_add(q, 0)
         store(LAST, 0, SLICE)
         main_add(LAST, 1)
         store(LAST, SLICE, SLICE)

@@ -7,6 +7,7 @@ FLOPS = 2 * 4096 * 1024 * 896
 
 F32 = mybir.dt.float32
 BF16 = mybir.dt.bfloat16
+I32 = mybir.dt.int32
 U32 = mybir.dt.uint32
 U8 = mybir.dt.uint8
 FP8X4 = mybir.dt.float8_e4m3fn_x4
@@ -14,77 +15,84 @@ ADD = mybir.AluOpType.add
 
 P = 128
 PACK = 4
+B = 2
+T = 8
+R = 16
+C = 16
 G = 2
-SLICE = 256
-CHUNK = 512
-N_PAIRS = 8
-LINE = 16
-BASE = 16
-SPLIT = 256
-WIDE_FROM = 3
-LOADS = [6, 5, 4, 0, 3, (0, 0, 1), 2, 1, (0, 1, 1), (1, 0, 1), (1, 1, 1), (2, 0, 1), (2, 1, 1), (3, 0, 1), (3, 1, 1), (4, 0, 2), (4, 1, 2), (6, 0, 2), (6, 1, 2)]
+SLICE = R * C
+ROW = B * C
+CHUNK = R * ROW
+GAP = 64
+PITCH = CHUNK + GAP
+S_ROWS = 16
+LOADS = [6, 5, (0, 2, 0, 0), 0, (0, 2, 0, 1), 4, 3, (0, 2, 1, 0), (0, 2, 1, 1), 2, 1, (2, 2, 0, 0), (2, 2, 0, 1), (2, 2, 1, 0), (2, 2, 1, 1), (4, 2, 0, 0), (4, 2, 0, 1), (4, 2, 1, 0), (4, 2, 1, 1), (6, 2, 0, 0), (6, 2, 0, 1), (6, 2, 1, 0), (6, 2, 1, 1)]
 HEAD = [
     ("wt", 6, 0),
-    ("wt", 5, 1),
-    ("wt", 4, 2),
-    ("wt", 0, 3),
-    ("wt", 3, 4),
-    ("wt", 2, 5),
-    ("wt", 1, 6),
+    ("wt", 5, 2),
+    ("wt", 0, 4),
+    ("wt", 4, 1),
+    ("wt", 3, 3),
     ("wc", 6),
     ("wc", 5),
-    ("wc", 4),
+    ("xc", "s", 1, 0, 0),
     ("wc", 0),
-    ("wc", 3),
     ("wq", 6),
+    ("xc", "v", 0, 0, 0),
     ("wq", 5),
-    ("wq", 4),
+    ("xc", "s", 0, 0, 1, 8, 16),
+    ("xc", "v", 0, 0, 1, 0, 8),
+    ("xc", "s", 1, 0, 1, 0, 8),
+    ("xc", "v", 1, 0, 1, 8, 16),
+    ("wc", 4),
+    ("wc", 3),
+    ("xq", 0, 0, 0, 8),
+    ("xq", 0, 0, 8, 16),
     ("wq", 0),
-    ("xc", 0, 0, 0, 256, 0),
+    ("xs", 0, 0),
+    ("xq", 1, 0),
+    ("mx", 0, 6, 0),
+    ("mx", 0, 5, 0),
+    ("mx", 0, 0, 0),
+    ("mx", 1, 6, 0),
+    ("mx", 1, 5, 0),
+    ("mx", 1, 0, 0),
+    ("wq", 4),
+    ("xs", 1, 0),
+    ("xc", "v", 0, 1, 0),
+    ("xc", "s", 1, 1, 0),
     ("wq", 3),
-    ("xq", 0, 0, 0, 256),
-    ("side", 0, 6, 0, 0, 256),
-    ("side", 0, 5, 0, 0, 256),
-    ("main", 0, 0, 4, 0),
-    ("main", 0, 0, 0, 0),
-    ("main", 0, 0, 3, 0),
-    ("xc", 0, 0, 256, 256, 256),
+    ("mx", 0, 4, 0),
+    ("mx", 1, 4, 0),
+    ("mx", 0, 3, 0),
+    ("mx", 1, 3, 0),
+    ("wt", 2, 6),
+    ("wt", 1, 7),
+    ("xc", "s", 0, 1, 1, 0, 8),
+    ("xc", "v", 0, 1, 1, 8, 16),
+    ("xc", "v", 1, 1, 1),
     ("wc", 2),
     ("wc", 1),
-    ("xq", 0, 0, 256, 256),
-    ("side", 0, 6, 0, 256, 256),
-    ("side", 0, 5, 0, 256, 256),
-    ("main", 0, 1, 4, 0),
-    ("main", 0, 1, 0, 0),
-    ("main", 0, 1, 3, 0),
+    ("xq", 0, 1),
+    ("xq", 1, 1),
+    ("xs", 0, 1),
+    ("xs", 1, 1),
     ("wq", 2),
-    ("main", 0, 0, 2, 0),
-    ("xc", 0, 1, 0, 256, 0),
-    ("xc", 0, 1, 256, 256, 256),
-    ("xq", 0, 1, 0, 256),
-    ("side", 0, 6, 1, 0, 256),
-    ("side", 0, 5, 1, 0, 256),
-    ("main", 0, 0, 4, 1),
-    ("main", 0, 0, 0, 1),
-    ("main", 0, 0, 3, 1),
     ("wq", 1),
-    ("main", 0, 1, 1, 0),
-    ("xc", 1, 0, 0, 512, 256),
-    ("xq", 0, 1, 256, 256),
-    ("side", 0, 6, 1, 256, 256),
-    ("side", 0, 5, 1, 256, 256),
-    ("main", 0, 1, 4, 1),
-    ("main", 0, 1, 0, 1),
-    ("main", 0, 1, 3, 1),
-    ("main", 0, 0, 2, 1),
-    ("main", 0, 1, 1, 1),
-    ("xc", 1, 1, 0, 512, 256),
-    ("xq", 1, 0, 0, 512),
-    ("xc", 2, 0, 0, 512, 256),
-    ("xq", 1, 1, 0, 512),
-    ("xc", 2, 1, 0, 512, 256),
-    ("xq", 2, 0, 0, 512),
-    ("xq", 2, 1, 0, 512),
+    ("mx", 0, 6, 1),
+    ("mx", 0, 5, 1),
+    ("mx", 0, 0, 1),
+    ("mx", 0, 4, 1),
+    ("mx", 0, 3, 1),
+    ("mx", 1, 6, 1),
+    ("mx", 1, 5, 1),
+    ("mx", 1, 0, 1),
+    ("mx", 1, 4, 1),
+    ("mx", 1, 3, 1),
+    ("mx", 0, 2, 0),
+    ("mx", 1, 1, 0),
+    ("mx", 0, 2, 1),
+    ("mx", 1, 1, 1),
 ]
 
 
@@ -93,43 +101,30 @@ def tile_stackeddirectionalconv3d_t_kernel(tc, x, W, out):
     with ExitStack() as ctx:
         ctx.enter_context(tc.manual_schedule())
         keep = ctx.enter_context(tc.tile_pool(name="keep", bufs=1))
-        stage = ctx.enter_context(tc.tile_pool(name="stage", bufs=3))
+        stage = ctx.enter_context(tc.tile_pool(name="stage", bufs=8))
         psum = ctx.enter_context(tc.psum_pool(name="psum", bufs=1))
 
-        x_codes = keep.tile([P, N_PAIRS, G, CHUNK], U32, name="x_codes", align_bytes=256)
-        x_scales = keep.tile([P, N_PAIRS, G, CHUNK], U8, name="x_scales", align_bytes=256)
+        x_codes = keep.tile([P, G, T + 1, PITCH], U32, name="x_codes", align_bytes=256)
+        x_scales = keep.tile([P, G, T + 1, PITCH], U8, name="x_scales", align_bytes=256)
+        x_scales_r = keep.tile([P, G, T + 1, PITCH], U8, name="x_scales_r", align_bytes=256)
         w_codes = keep.tile([P, 7, G * P], U32, name="w_codes", align_bytes=256)
         w_scales = keep.tile([P, 7, G * P], U8, name="w_scales", align_bytes=256)
-        zero_bf = keep.tile([P, P * PACK], BF16, name="zero_bf", align_bytes=64)
-        zero_codes = keep.tile([P, P], U32, name="zero_codes", align_bytes=64)
-        zero_scales = keep.tile([P, P], U8, name="zero_scales", align_bytes=64)
         ident = keep.tile([P, P], F32, name="ident")
-        res = keep.tile([P, N_PAIRS, CHUNK], F32, name="res")
+        res = keep.tile([P, T, B, R, C], F32, name="res")
 
         w_raw = {}
         x_raw = {}
-        wide = {}
 
         def load_w(k):
             w_raw[k] = keep.tile([P, 1024], BF16, name="w_raw%d" % k)
             nc.sync.dma_start(out=w_raw[k][:], in_=W[P * k : P * (k + 1), :])
 
-        x_tiles = {}
-
-        def load_x(q, g, m, c0=0, n=CHUNK):
-            if (q, m) not in x_tiles:
-                x_tiles[(q, m)] = keep.tile([P, G, PACK, m * CHUNK], BF16, name="x_raw_%d" % q)
-            t = x_tiles[(q, m)]
-            for i in range(m):
-                x_raw[(q + i, g)] = t[:, g, :, CHUNK * i : CHUNK * (i + 1)]
-                wide[q + i] = t[:, :, :, CHUNK * i : CHUNK * (i + 1)]
-            b, qq = divmod(q, 4)
-            xb = x[b].rearrange("k t r c -> k (t r c)")
-            width = m * CHUNK if m > 1 else n
-            rows = xb[512 * g : 512 * g + 512, CHUNK * qq + c0 : CHUNK * qq + c0 + width]
-            nc.sync.dma_start(
-                out=t[:, g, :, c0 : c0 + width], in_=rows.rearrange("(p e) w -> p e w", e=PACK)
-            )
+        def load_x(t, n, g, b):
+            tile = keep.tile([P, PACK, n * SLICE], BF16, name="x_raw_%d_%d_%d" % (t, g, b))
+            for i in range(n):
+                x_raw[(t + i, g, b)] = tile[:, :, SLICE * i : SLICE * (i + 1)]
+            rows = x[b].rearrange("k t r c -> k (t r c)")[512 * g : 512 * (g + 1), SLICE * t : SLICE * (t + n)]
+            nc.sync.dma_start(out=tile[:], in_=rows.rearrange("(p e) w -> p e w", e=PACK))
 
         for item in LOADS:
             if isinstance(item, int):
@@ -137,13 +132,11 @@ def tile_stackeddirectionalconv3d_t_kernel(tc, x, W, out):
             else:
                 load_x(*item)
 
-        def lines(ap):
-            return ap.rearrange("p (l c) -> p l c", c=LINE)
-
         make_identity(nc, ident[:])
-        nc.vector.memset(zero_bf[:], 0.0)
-        nc.vector.quantize_mx(out=zero_codes[:].bitcast(FP8X4), scales=zero_scales[:], in_=zero_bf[:])
-        nc.gpsimd.memset(res[:].rearrange("p q (l c) -> p (q l) c", c=LINE)[:, :, LINE - 1 : LINE], 0.0)
+        nc.gpsimd.memset(x_codes[:].bitcast(I32)[:, :, :, 0:GAP], 0)
+        for plane in (x_scales, x_scales_r):
+            nc.vector.memset(plane[:].rearrange("p g t w -> p (g t w)").bitcast(I32), 0)
+        nc.gpsimd.memset(res[:].rearrange("p t b r c -> p (t b r) c")[:, :, C - 1 : C], 0.0)
 
         def bank(i, name):
             return psum.tile([P, 512], F32, name=name, tag="bank%d" % i)
@@ -177,170 +170,160 @@ def tile_stackeddirectionalconv3d_t_kernel(tc, x, W, out):
 
         grouped = {}
 
-        def runs4(ap, order):
-            return ap.rearrange(order, i=4)
+        def xc_(e, t, g, b, r0=0, r1=R):
+            if (t, g) not in grouped:
+                grouped[(t, g)] = stage.tile([P, R, B, C, PACK], BF16, name="grouped", align_bytes=64)
+            dst = grouped[(t, g)][:, r0:r1, b, :, :].rearrange("p r (c i) t -> p r c t i", i=4)
+            src = x_raw[(t, g, b)][:, :, C * r0 : C * r1].rearrange("p t (r c i) -> p r c t i", c=4, i=4)
+            if e == "s":
+                nc.scalar.copy(out=dst, in_=src)
+            else:
+                nc.vector.tensor_copy(out=dst, in_=src)
 
-        def xc_(q, g, c0, n, s):
-            t = stage.tile([P, CHUNK, PACK], BF16, name="grouped", align_bytes=64)
-            grouped[(q, g, c0)] = t
-            raw = x_raw[(q, g)]
-            if s > 0:
-                nc.scalar.copy(
-                    out=runs4(t[:, 0:s, :], "p (c i) t -> p c t i"),
-                    in_=runs4(raw[:, :, c0 : c0 + s], "p t (c i) -> p c t i"),
-                )
-            if s < n:
-                nc.vector.tensor_copy(
-                    out=runs4(t[:, s:n, :], "p (c i) t -> p c t i"),
-                    in_=runs4(raw[:, :, c0 + s : c0 + n], "p t (c i) -> p c t i"),
-                )
-
-        def xq_(q, g, c0, n):
+        def xq_(t, g, r0=0, r1=R):
+            lo, hi = GAP + ROW * r0, GAP + ROW * r1
             nc.vector.quantize_mx(
-                out=x_codes[:, q, g, c0 : c0 + n].bitcast(FP8X4),
-                scales=x_scales[:, q, g, c0 : c0 + n],
-                in_=grouped[(q, g, c0)][:, 0:n, :].rearrange("p w j -> p (w j)"),
+                out=x_codes[:, g, t, lo:hi].bitcast(FP8X4),
+                scales=x_scales[:, g, t, lo:hi],
+                in_=grouped[(t, g)][:, r0:r1, :, :, :].rearrange("p r b c t -> p (r b c t)"),
             )
 
-        def pair_tile(q):
-            grouped[q] = stage.tile([P, G, CHUNK, PACK], BF16, name="grouped2", align_bytes=64)
+        def flat(tile, g):
+            return tile[:, g, :, :].rearrange("p t w -> p (t w)")
 
-        def pair_s(q, g):
-            nc.scalar.copy(
-                out=runs4(grouped[q][:, g, 0:SPLIT, :], "p (c i) t -> p c t i"),
-                in_=runs4(wide[q][:, g, :, 0:SPLIT], "p t (c i) -> p c t i"),
+        def xs_(t, g, n=1):
+            lo = PITCH * t + GAP
+            nc.vector.tensor_copy(
+                out=flat(x_scales_r, g).bitcast(I32)[:, (lo + ROW) // 4 : (lo + ROW + CHUNK) // 4],
+                in_=flat(x_scales, g).bitcast(I32)[:, lo // 4 : (lo + CHUNK) // 4],
             )
 
-        def pair_v(q):
-            for g in range(G):
-                nc.vector.tensor_copy(
-                    out=runs4(grouped[q][:, g, SPLIT:CHUNK, :], "p (c i) t -> p c t i"),
-                    in_=runs4(wide[q][:, g, :, SPLIT:CHUNK], "p t (c i) -> p c t i"),
-                )
-
-        def pair_q(q):
-            nc.vector.quantize_mx(
-                out=x_codes[:, q, :, :].rearrange("p g c -> p (g c)").bitcast(FP8X4),
-                scales=x_scales[:, q, :, :].rearrange("p g c -> p (g c)"),
-                in_=grouped[q][:].rearrange("p g w j -> p (g w j)"),
-            )
-
-        SHIFT = {4: (-LINE, 0), 0: (0, 0), 3: (LINE, 0), 1: (0, -1), 2: (0, 1)}
+        SHIFT = {6: ("a", 0, 0), 5: ("b", 0, 0), 0: ("m", 0, 0), 4: ("m", 1, 0), 3: ("m", -1, 0), 1: ("m", 0, -1), 2: ("m", 0, 1)}
+        BANKS = {"a": (0, 1), "b": (2, 3), "m": (4, 5, 6, 7)}
         banks = {}
         done = {}
 
-        def valid(s, k):
-            return 0 <= s % 8 + SHIFT[k][1] <= 7
+        def valid(t, k):
+            return 0 <= t + SHIFT[k][2] < T
 
-        def mx(key, lo, n, k, g, rhs, rhs_scale, total):
+        def mx(t, k, g, r0=0, r1=R):
+            if not valid(t, k):
+                return
+            which, dr, dt = SHIFT[k]
+            key = (which, t, r0)
             if key not in banks:
-                banks[key] = bank(4 * (key[0] % 2) + key[1], "acc%d" % key[1])
+                slot = t if r0 == 0 else t + 1
+                banks[key] = bank(BANKS[which][slot % len(BANKS[which])], "acc_%s" % which)
+            total = G * sum(1 for j in SHIFT if SHIFT[j][0] == which and valid(t, j))
             i = done.get(key, 0)
-            done[key] = i + n
+            done[key] = i + 1
+            lo = PITCH * (t + dt) + GAP + ROW * (r0 + dr)
+            n = ROW * (r1 - r0)
+            codes = flat(x_codes, g)[:, lo : lo + n]
+            scales = flat(x_scales, g)[:, lo : lo + n] if dr == 0 else flat(x_scales_r, g)[:, lo + ROW : lo + ROW + n]
             nc.tensor.matmul_mx(
-                out=banks[key][:, lo : lo + n],
+                out=banks[key][:, 0:n],
                 lhsT=w_codes[:, k, P * g : P * (g + 1)].bitcast(FP8X4),
                 lhsT_scale=w_scales[:, k, P * g : P * (g + 1)],
-                rhs=rhs.bitcast(FP8X4),
-                rhs_scale=rhs_scale,
+                rhs=codes.bitcast(FP8X4),
+                rhs_scale=scales,
                 start=(i == 0),
-                stop=(i + n == total),
+                stop=(i == total - 1),
             )
 
-        def x_cols(q, g, c0, n):
-            return x_codes[:, q, g, c0 : c0 + n], x_scales[:, q, g, c0 : c0 + n]
+        def bank_rows(which, t, r0=0):
+            return banks[(which, t, r0)][:].rearrange("p (r b c) -> p r b c", b=B, c=C)
 
-        def side(q, k, g, c0=0, n=CHUNK):
-            mx((q, 0 if k == 6 else 1), c0, n, k, g, *x_cols(q, g, c0, n), G * CHUNK)
+        def res_rows(t):
+            return res[:, t, :, :, :].rearrange("p b r c -> p r b c")
 
-        def main(q, h, k, g):
-            s = 2 * q + h
-            if not valid(s, k):
-                return
-            total = P + SLICE * G * sum(valid(s, j) for j in SHIFT)
-            shift, d = SHIFT[k]
-            xs = s + d
-            key = (q, 2 + h)
-            mx(key, BASE + shift, SLICE, k, g, *x_cols(xs // 2, g, SLICE * (xs % 2), SLICE), total)
-            if k == 4 and key not in marked:
-                marked.add(key)
-                mx(key, SLICE, P, k, g, zero_codes[:], zero_scales[:], total)
+        def side_copy(t):
+            nc.scalar.copy(out=res_rows(t)[:, :, :, 0 : C - 1], in_=bank_rows("a", t)[:, :, :, 1:C])
 
-        marked = set()
+        def side_add(t):
+            dst = res_rows(t)[:, :, :, 1:C]
+            nc.vector.tensor_tensor(out=dst, in0=dst, in1=bank_rows("b", t)[:, :, :, 0 : C - 1], op=ADD)
 
-        def side_copy(q):
-            nc.scalar.copy(
-                out=lines(res[:, q, :])[:, :, 0 : LINE - 1], in_=lines(banks[(q, 0)][:])[:, :, 1:LINE]
+        def main_add(t, r0=0, r1=R):
+            dst = res_rows(t)[:, r0:r1]
+            nc.vector.tensor_tensor(out=dst, in0=dst, in1=bank_rows("m", t, r0)[:, 0 : r1 - r0], op=ADD)
+
+        def store(t, r0=0, r1=R):
+            o = out.rearrange("b o t r c -> o b t (r c)")
+            nc.sync.dma_start(
+                out=o[:, :, t, C * r0 : C * r1],
+                in_=res[:, t, :, r0:r1, :].rearrange("p b r c -> p b (r c)"),
             )
 
-        def side_add(q):
-            dst = lines(res[:, q, :])[:, :, 1:LINE]
-            nc.vector.tensor_tensor(out=dst, in0=dst, in1=lines(banks[(q, 1)][:])[:, :, 0 : LINE - 1], op=ADD)
-
-        def main_add(q, h):
-            cols = slice(SLICE * h, SLICE * (h + 1))
-            nc.vector.tensor_tensor(
-                out=res[:, q, cols], in0=res[:, q, cols], in1=banks[(q, 2 + h)][:, BASE : BASE + SLICE], op=ADD
-            )
-
-        def store(q, lo, n):
-            b, qq = divmod(q, 4)
-            ob = out[b].rearrange("o t r c -> o (t r c)")
-            nc.sync.dma_start(out=ob[:, CHUNK * qq + lo : CHUNK * qq + lo + n], in_=res[:, q, lo : lo + n])
-
-        acts = {"wt": wt_, "wc": wc_, "wq": wq_, "xc": xc_, "xq": xq_, "side": side, "main": main}
+        acts = {"wt": wt_, "wc": wc_, "wq": wq_, "xc": xc_, "xq": xq_, "mx": mx, "xs": xs_}
         for step in HEAD:
             acts[step[0]](*step[1:])
 
-        LAST = N_PAIRS - 1
-        FINE = 2
+        LAST = T - 1
+        HALF = R // 2
 
-        def tail_of(q):
-            for g in range(G):
-                main(q, 1, 2, g)
+        def xs(t, g):
+            if t < T:
+                xc_("s", t, g, 0)
+                xc_("s", t, g, 1, 0, 1)
 
-        def body(q):
-            for g in range(G):
-                for k in (6, 5):
-                    side(q, k, g)
-            for h in range(2):
-                for k in (4, 0, 3, 1, 2) if h == 0 else (4, 0, 3, 1):
-                    for g in range(G):
-                        main(q, h, k, g)
+        def xv(t, g):
+            if t < T:
+                xc_("v", t, g, 1, 1, R)
 
-        def body_fine(q):
-            for g in range(G):
-                main(q - 1, 1, 2, g)
-                for k in (6, 5):
-                    side(q, k, g)
-                for h in range(2):
-                    for k in (4, 0, 3, 1, 2) if h == 0 else (4, 0, 3, 1):
-                        main(q, h, k, g)
+        def quant(t, g):
+            if t < T:
+                xq_(t, g)
 
-        for q in range(N_PAIRS):
-            ahead = q + 2
-            prep = WIDE_FROM <= ahead < N_PAIRS
-            if q >= 1:
-                if q < FINE:
-                    body_fine(q)
-                else:
-                    tail_of(q - 1)
-                    body(q)
-            if prep:
-                pair_tile(ahead)
-                pair_s(ahead, 0)
-            side_copy(q)
-            if prep:
-                pair_s(ahead, 1)
-            if q >= 1:
-                main_add(q - 1, 1)
-                store(q - 1, 0, CHUNK)
-            if prep:
-                pair_v(ahead)
-            side_add(q)
-            if prep:
-                pair_q(ahead)
-            main_add(q, 0)
-        store(LAST, 0, SLICE)
-        main_add(LAST, 1)
-        store(LAST, SLICE, SLICE)
+        def scale(t, g):
+            if t < T:
+                xs_(t, g)
+
+        for e in range(0, T, 2):
+            o = e + 1
+            if e > 0:
+                for g in range(G):
+                    sides_first = g == 1
+                    mx(e - 1, 2, g)
+                    if sides_first:
+                        for t in (e, o):
+                            for k in (6, 5):
+                                mx(t, k, g)
+                    for t in (e, o):
+                        if t == o:
+                            mx(e, 2, g)
+                        if not sides_first:
+                            for k in (6, 5):
+                                mx(t, k, g)
+                        for r0 in (0, HALF) if t == LAST else (0,):
+                            for k in (0, 1, 4, 3):
+                                mx(t, k, g, r0, r0 + HALF if t == LAST else R)
+            a, b = e + 2, e + 3
+            xs(a, 0)
+            side_copy(e)
+            side_copy(o)
+            xs(b, 0)
+            xs(a, 1)
+            xs(b, 1)
+            xv(a, 0)
+            xv(b, 0)
+            quant(a, 0)
+            if e > 0:
+                main_add(e - 1)
+                store(e - 1)
+            side_add(e)
+            side_add(o)
+            scale(a, 0)
+            quant(b, 0)
+            main_add(e)
+            store(e)
+            xv(a, 1)
+            scale(b, 0)
+            xv(b, 1)
+            quant(a, 1)
+            scale(a, 1)
+            quant(b, 1)
+            scale(b, 1)
+        for r0 in (0, HALF):
+            main_add(LAST, r0, r0 + HALF)
+            store(LAST, r0, r0 + HALF)

@@ -134,8 +134,8 @@ def tile_stackeddirectionalconv3d_t_kernel(tc, x, W, out):
 
         make_identity(nc, ident[:])
         nc.gpsimd.memset(x_codes[:].bitcast(I32)[:, :, :, 0:GAP], 0)
-        for plane in (x_scales, x_scales_r):
-            nc.vector.memset(plane[:].rearrange("p g t w -> p (g t w)").bitcast(I32), 0)
+        nc.vector.memset(x_scales[:].rearrange("p g t w -> p (g t w)").bitcast(I32), 0)
+        nc.gpsimd.memset(x_scales_r[:].bitcast(I32)[:, :, :, ROW // 4 : (ROW + GAP) // 4], 0)
         nc.gpsimd.memset(res[:].rearrange("p t b r c -> p (t b r) c")[:, :, C - 1 : C], 0.0)
 
         def bank(i, name):
@@ -265,11 +265,11 @@ def tile_stackeddirectionalconv3d_t_kernel(tc, x, W, out):
         def xs(t, g):
             if t < T:
                 xc_("s", t, g, 0)
-                xc_("s", t, g, 1, 0, 1)
+                xc_("s", t, g, 1, 0, 2)
 
         def xv(t, g):
             if t < T:
-                xc_("v", t, g, 1, 1, R)
+                xc_("v", t, g, 1, 2, R)
 
         def quant(t, g):
             if t < T:

@@ -28,9 +28,11 @@ PITCH = CHUNK + GAP
 S_ROWS = 16
 LOADS = [6, 5, (0, 2, 0, 0), 0, (0, 2, 0, 1), 4, 3, (0, 2, 1, 0), (0, 2, 1, 1), 2, 1, (2, 2, 0, 0), (2, 2, 0, 1), (2, 2, 1, 0), (2, 2, 1, 1), (4, 2, 0, 0), (4, 2, 0, 1), (4, 2, 1, 0), (4, 2, 1, 1), (6, 2, 0, 0), (6, 2, 0, 1), (6, 2, 1, 0), (6, 2, 1, 1)]
 HEAD = [
+    ("idle", 4),
     ("wt", 6, 0),
     ("wt", 5, 2),
     ("wt", 0, 4),
+    ("idle", 3),
     ("wt", 4, 1),
     ("wt", 3, 3),
     ("wc", 6),
@@ -134,12 +136,19 @@ def tile_stackeddirectionalconv3d_t_kernel(tc, x, W, out):
 
         make_identity(nc, ident[:])
         nc.gpsimd.memset(x_codes[:].bitcast(I32)[:, :, :, 0:GAP], 0)
+        zero = keep.tile([P, 512], BF16, name="zero")
+        nc.vector.memset(zero[:], 0.0)
         nc.vector.memset(x_scales[:].rearrange("p g t w -> p (g t w)").bitcast(I32), 0)
         nc.gpsimd.memset(x_scales_r[:].bitcast(I32)[:, :, :, ROW // 4 : (ROW + GAP) // 4], 0)
         nc.gpsimd.memset(res[:].rearrange("p t b r c -> p (t b r) c")[:, :, C - 1 : C], 0.0)
 
         def bank(i, name):
             return psum.tile([P, 512], F32, name=name, tag="bank%d" % i)
+
+        def idle_(n):
+            unread = bank(5, "unread")
+            for j in range(n):
+                nc.tensor.matmul(unread[:], lhsT=zero[:, 0:P], rhs=zero[:], start=True, stop=True)
 
         wt = {}
 
@@ -255,7 +264,7 @@ def tile_stackeddirectionalconv3d_t_kernel(tc, x, W, out):
                 in_=res[:, t, :, r0:r1, :].rearrange("p b r c -> p b (r c)"),
             )
 
-        acts = {"wt": wt_, "wc": wc_, "wq": wq_, "xc": xc_, "xq": xq_, "mx": mx, "xs": xs_}
+        acts = {"idle": idle_, "wt": wt_, "wc": wc_, "wq": wq_, "xc": xc_, "xq": xq_, "mx": mx, "xs": xs_}
         for step in HEAD:
             acts[step[0]](*step[1:])
 

@@ -274,11 +274,11 @@ def tile_stackeddirectionalconv3d_t_kernel(tc, x, W, out):
         def xs(t, g):
             if t < T:
                 xc_("s", t, g, 0)
-                xc_("s", t, g, 1, 0, 2)
+
 
         def xv(t, g):
             if t < T:
-                xc_("v", t, g, 1, 2, R)
+                xc_("v", t, g, 1, 0, R)
 
         def quant(t, g):
             if t < T:
@@ -330,8 +330,8 @@ def tile_stackeddirectionalconv3d_t_kernel(tc, x, W, out):
             scale(b, 0)
             xv(b, 1)
             quant(a, 1)
-            scale(a, 1)
             quant(b, 1)
+            scale(a, 1)
             scale(b, 1)
         for r0 in (0, HALF):
             main_add(LAST, r0, r0 + HALF)

from contextlib import ExitStack

import concourse.mybir as mybir
from concourse.masks import make_identity

FLOPS = 2 * 4096 * 1024 * 896

F32 = mybir.dt.float32
BF16 = mybir.dt.bfloat16
I32 = mybir.dt.int32
U32 = mybir.dt.uint32
U8 = mybir.dt.uint8
FP8X4 = mybir.dt.float8_e4m3fn_x4
ADD = mybir.AluOpType.add

P = 128
PACK = 4
B = 2
T = 8
R = 16
C = 16
G = 2
SLICE = R * C
ROW = B * C
CHUNK = R * ROW
GAP = 64
PITCH = CHUNK + GAP
S_ROWS = 16
LOADS = [6, 5, (0, 2, 0, 0), 0, (0, 2, 0, 1), 4, 3, (0, 2, 1, 0), (0, 2, 1, 1), 2, 1, (2, 2, 0, 0), (2, 2, 0, 1), (2, 2, 1, 0), (2, 2, 1, 1), (4, 2, 0, 0), (4, 2, 0, 1), (4, 2, 1, 0), (4, 2, 1, 1), (6, 2, 0, 0), (6, 2, 0, 1), (6, 2, 1, 0), (6, 2, 1, 1)]
HEAD = [
    ("idle", 4),
    ("wt", 6, 0),
    ("wt", 5, 2),
    ("wt", 0, 4),
    ("idle", 3),
    ("wt", 4, 1),
    ("wt", 3, 3),
    ("wc", 6),
    ("wc", 5),
    ("xc", "s", 1, 0, 0),
    ("wc", 0),
    ("wq", 6),
    ("xc", "v", 0, 0, 0),
    ("wq", 5),
    ("xc", "s", 0, 0, 1, 8, 16),
    ("xc", "v", 0, 0, 1, 0, 8),
    ("xc", "s", 1, 0, 1, 0, 8),
    ("xc", "v", 1, 0, 1, 8, 16),
    ("wc", 4),
    ("wc", 3),
    ("xq", 0, 0, 0, 8),
    ("xq", 0, 0, 8, 16),
    ("wq", 0),
    ("xs", 0, 0),
    ("xq", 1, 0),
    ("mx", 0, 6, 0),
    ("mx", 0, 5, 0),
    ("mx", 0, 0, 0),
    ("mx", 1, 6, 0),
    ("mx", 1, 5, 0),
    ("mx", 1, 0, 0),
    ("wq", 4),
    ("xs", 1, 0),
    ("xc", "v", 0, 1, 0),
    ("xc", "s", 1, 1, 0),
    ("wq", 3),
    ("mx", 0, 4, 0),
    ("mx", 1, 4, 0),
    ("mx", 0, 3, 0),
    ("mx", 1, 3, 0),
    ("wt", 2, 6),
    ("wt", 1, 7),
    ("xc", "s", 0, 1, 1, 0, 8),
    ("xc", "v", 0, 1, 1, 8, 16),
    ("xc", "v", 1, 1, 1),
    ("wc", 2),
    ("wc", 1),
    ("xq", 0, 1),
    ("xq", 1, 1),
    ("xs", 0, 1),
    ("xs", 1, 1),
    ("wq", 2),
    ("wq", 1),
    ("mx", 0, 6, 1),
    ("mx", 0, 5, 1),
    ("mx", 0, 0, 1),
    ("mx", 0, 4, 1),
    ("mx", 0, 3, 1),
    ("mx", 1, 6, 1),
    ("mx", 1, 5, 1),
    ("mx", 1, 0, 1),
    ("mx", 1, 4, 1),
    ("mx", 1, 3, 1),
    ("mx", 0, 2, 0),
    ("mx", 1, 1, 0),
    ("mx", 0, 2, 1),
    ("mx", 1, 1, 1),
]


def tile_stackeddirectionalconv3d_t_kernel(tc, x, W, out):
    nc = tc.nc
    with ExitStack() as ctx:
        ctx.enter_context(tc.manual_schedule())
        keep = ctx.enter_context(tc.tile_pool(name="keep", bufs=1))
        stage = ctx.enter_context(tc.tile_pool(name="stage", bufs=8))
        psum = ctx.enter_context(tc.psum_pool(name="psum", bufs=1))

        x_codes = keep.tile([P, G, T + 1, PITCH], U32, name="x_codes", align_bytes=256)
        x_scales = keep.tile([P, G, T + 1, PITCH], U8, name="x_scales", align_bytes=256)
        x_scales_r = keep.tile([P, G, T + 1, PITCH], U8, name="x_scales_r", align_bytes=256)
        w_codes = keep.tile([P, 7, G * P], U32, name="w_codes", align_bytes=256)
        w_scales = keep.tile([P, 7, G * P], U8, name="w_scales", align_bytes=256)
        ident = keep.tile([P, P], F32, name="ident")
        res = keep.tile([P, T, B, R, C], F32, name="res")

        w_raw = {}
        x_raw = {}

        def load_w(k):
            w_raw[k] = keep.tile([P, 1024], BF16, name="w_raw%d" % k)
            nc.sync.dma_start(out=w_raw[k][:], in_=W[P * k : P * (k + 1), :])

        def load_x(t, n, g, b):
            tile = keep.tile([P, PACK, n * SLICE], BF16, name="x_raw_%d_%d_%d" % (t, g, b))
            for i in range(n):
                x_raw[(t + i, g, b)] = tile[:, :, SLICE * i : SLICE * (i + 1)]
            rows = x[b].rearrange("k t r c -> k (t r c)")[512 * g : 512 * (g + 1), SLICE * t : SLICE * (t + n)]
            nc.sync.dma_start(out=tile[:], in_=rows.rearrange("(p e) w -> p e w", e=PACK))

        for item in LOADS:
            if isinstance(item, int):
                load_w(item)
            else:
                load_x(*item)

        make_identity(nc, ident[:])
        nc.gpsimd.memset(x_codes[:].bitcast(I32)[:, :, :, 0:GAP], 0)
        zero = keep.tile([P, 512], BF16, name="zero")
        nc.vector.memset(zero[:], 0.0)
        nc.vector.memset(x_scales[:].rearrange("p g t w -> p (g t w)").bitcast(I32), 0)
        nc.gpsimd.memset(x_scales_r[:].bitcast(I32)[:, :, :, ROW // 4 : (ROW + GAP) // 4], 0)
        nc.gpsimd.memset(res[:].rearrange("p t b r c -> p (t b r) c")[:, :, C - 1 : C], 0.0)

        def bank(i, name):
            return psum.tile([P, 512], F32, name=name, tag="bank%d" % i)

        def idle_(n):
            unread = bank(5, "unread")
            for j in range(n):
                nc.tensor.matmul(unread[:], lhsT=zero[:, 0:P], rhs=zero[:], start=True, stop=True)

        wt = {}

        def wt_(k, i):
            words = w_raw[k][:].bitcast(F32)
            wt[k] = bank(i, "wt%d" % k)
            for j in range(4):
                g, u = divmod(j, 2)
                nc.tensor.transpose(
                    wt[k][:, P * j : P * (j + 1)], words[:, 256 * g + u : 256 * (g + 1) : 2], ident[:]
                )

        w_grouped = {}

        def wc_(k, e="s"):
            w_grouped[k] = keep.tile([P, G * P * PACK], BF16, name="w_grouped%d" % k, align_bytes=64)
            dst = w_grouped[k][:].bitcast(F32).rearrange("p (g o u) -> p g o u", g=G, u=2)
            src = wt[k][:].rearrange("p (g u o) -> p g o u", g=G, u=2)
            if e == "s":
                nc.scalar.copy(out=dst, in_=src)
            else:
                nc.vector.tensor_copy(out=dst, in_=src)

        def wq_(k):
            nc.vector.quantize_mx(
                out=w_codes[:, k, :].bitcast(FP8X4), scales=w_scales[:, k, :], in_=w_grouped[k][:]
            )

        grouped = {}

        def xc_(e, t, g, b, r0=0, r1=R):
            if (t, g) not in grouped:
                grouped[(t, g)] = stage.tile([P, R, B, C, PACK], BF16, name="grouped", align_bytes=64)
            dst = grouped[(t, g)][:, r0:r1, b, :, :].rearrange("p r (c i) t -> p r c t i", i=4)
            src = x_raw[(t, g, b)][:, :, C * r0 : C * r1].rearrange("p t (r c i) -> p r c t i", c=4, i=4)
            if e == "s":
                nc.scalar.copy(out=dst, in_=src)
            else:
                nc.vector.tensor_copy(out=dst, in_=src)

        def xq_(t, g, r0=0, r1=R):
            lo, hi = GAP + ROW * r0, GAP + ROW * r1
            nc.vector.quantize_mx(
                out=x_codes[:, g, t, lo:hi].bitcast(FP8X4),
                scales=x_scales[:, g, t, lo:hi],
                in_=grouped[(t, g)][:, r0:r1, :, :, :].rearrange("p r b c t -> p (r b c t)"),
            )

        def flat(tile, g):
            return tile[:, g, :, :].rearrange("p t w -> p (t w)")

        def xs_(t, g, n=1):
            lo = PITCH * t + GAP
            nc.vector.tensor_copy(
                out=flat(x_scales_r, g).bitcast(I32)[:, (lo + ROW) // 4 : (lo + ROW + CHUNK) // 4],
                in_=flat(x_scales, g).bitcast(I32)[:, lo // 4 : (lo + CHUNK) // 4],
            )

        SHIFT = {6: ("a", 0, 0), 5: ("b", 0, 0), 0: ("m", 0, 0), 4: ("m", 1, 0), 3: ("m", -1, 0), 1: ("m", 0, -1), 2: ("m", 0, 1)}
        BANKS = {"a": (0, 1), "b": (2, 3), "m": (4, 5, 6, 7)}
        banks = {}
        done = {}

        def valid(t, k):
            return 0 <= t + SHIFT[k][2] < T

        def mx(t, k, g, r0=0, r1=R):
            if not valid(t, k):
                return
            which, dr, dt = SHIFT[k]
            key = (which, t, r0)
            if key not in banks:
                slot = t if r0 == 0 else t + 1
                banks[key] = bank(BANKS[which][slot % len(BANKS[which])], "acc_%s" % which)
            total = G * sum(1 for j in SHIFT if SHIFT[j][0] == which and valid(t, j))
            i = done.get(key, 0)
            done[key] = i + 1
            lo = PITCH * (t + dt) + GAP + ROW * (r0 + dr)
            n = ROW * (r1 - r0)
            codes = flat(x_codes, g)[:, lo : lo + n]
            scales = flat(x_scales, g)[:, lo : lo + n] if dr == 0 else flat(x_scales_r, g)[:, lo + ROW : lo + ROW + n]
            nc.tensor.matmul_mx(
                out=banks[key][:, 0:n],
                lhsT=w_codes[:, k, P * g : P * (g + 1)].bitcast(FP8X4),
                lhsT_scale=w_scales[:, k, P * g : P * (g + 1)],
                rhs=codes.bitcast(FP8X4),
                rhs_scale=scales,
                start=(i == 0),
                stop=(i == total - 1),
            )

        def bank_rows(which, t, r0=0):
            return banks[(which, t, r0)][:].rearrange("p (r b c) -> p r b c", b=B, c=C)

        def res_rows(t):
            return res[:, t, :, :, :].rearrange("p b r c -> p r b c")

        def side_copy(t):
            nc.scalar.copy(out=res_rows(t)[:, :, :, 0 : C - 1], in_=bank_rows("a", t)[:, :, :, 1:C])

        def side_add(t):
            dst = res_rows(t)[:, :, :, 1:C]
            nc.vector.tensor_tensor(out=dst, in0=dst, in1=bank_rows("b", t)[:, :, :, 0 : C - 1], op=ADD)

        def main_add(t, r0=0, r1=R):
            dst = res_rows(t)[:, r0:r1]
            nc.vector.tensor_tensor(out=dst, in0=dst, in1=bank_rows("m", t, r0)[:, 0 : r1 - r0], op=ADD)

        def store(t, r0=0, r1=R):
            o = out.rearrange("b o t r c -> o b t (r c)")
            nc.sync.dma_start(
                out=o[:, :, t, C * r0 : C * r1],
                in_=res[:, t, :, r0:r1, :].rearrange("p b r c -> p b (r c)"),
            )

        acts = {"idle": idle_, "wt": wt_, "wc": wc_, "wq": wq_, "xc": xc_, "xq": xq_, "mx": mx, "xs": xs_}
        for step in HEAD:
            acts[step[0]](*step[1:])

        LAST = T - 1
        HALF = R // 2

        def xs(t, g):
            if t < T:
                xc_("s", t, g, 0)


        def xv(t, g):
            if t < T:
                xc_("v", t, g, 1, 0, R)

        def quant(t, g):
            if t < T:
                xq_(t, g)

        def scale(t, g):
            if t < T:
                xs_(t, g)

        for e in range(0, T, 2):
            o = e + 1
            if e > 0:
                for g in range(G):
                    sides_first = g == 1
                    mx(e - 1, 2, g)
                    if sides_first:
                        for t in (e, o):
                            for k in (6, 5):
                                mx(t, k, g)
                    for t in (e, o):
                        if t == o:
                            mx(e, 2, g)
                        if not sides_first:
                            for k in (6, 5):
                                mx(t, k, g)
                        for r0 in (0, HALF) if t == LAST else (0,):
                            for k in (0, 1, 4, 3):
                                mx(t, k, g, r0, r0 + HALF if t == LAST else R)
            a, b = e + 2, e + 3
            xs(a, 0)
            side_copy(e)
            side_copy(o)
            xs(b, 0)
            xs(a, 1)
            xs(b, 1)
            xv(a, 0)
            xv(b, 0)
            quant(a, 0)
            if e > 0:
                main_add(e - 1)
                store(e - 1)
            side_add(e)
            side_add(o)
            scale(a, 0)
            quant(b, 0)
            main_add(e)
            store(e)
            xv(a, 1)
            scale(b, 0)
            xv(b, 1)
            quant(a, 1)
            quant(b, 1)
            scale(a, 1)
            scale(b, 1)
        for r0 in (0, HALF):
            main_add(LAST, r0, r0 + HALF)
            store(LAST, r0, r0 + HALF)
